import numpy as np
import ml_dtypes


def mxq(x, axis, fmt="e4m3"):
    dtype, down = {"e4m3": (ml_dtypes.float8_e4m3fn, 7), "e5m2": (ml_dtypes.float8_e5m2, 14)}[fmt]
    v = np.moveaxis(np.asarray(x, np.float32).astype(ml_dtypes.bfloat16).astype(np.float64), axis, -1)
    blocks = v.reshape(v.shape[:-1] + (-1, 32))
    amax = np.abs(blocks).max(-1, keepdims=True)
    byte = np.maximum(np.where(amax > 0, np.frexp(amax)[1] - 1 + 127, 0) - down, 1)
    scale = np.exp2(byte - 127.0)
    codes = (blocks / scale).astype(np.float32).astype(dtype).astype(np.float64)
    return np.moveaxis((codes * scale).reshape(v.shape), -1, axis)


WIDE = False


def mx_kscale(k):
    if not WIDE:
        return np.ones(k)
    levels = np.array([30, -30])
    if k % 512:
        return np.exp2(np.random.permutation(np.resize(levels, k // 32))).repeat(32)
    a = np.empty((k // 512, 16))
    for p in range(k // 512):
        a[p, :8] = np.random.permutation(np.resize(levels, 8))
        for g in range(8):
            far = levels[np.abs(levels - a[p, g]) >= 10]
            a[p, g + 8] = far[np.random.randint(len(far))]
    return np.exp2(a.ravel()).repeat(32)


BF16 = ml_dtypes.bfloat16


def bf(x):
    return np.asarray(x, np.float32).astype(BF16)


def f64(x):
    return np.asarray(x).astype(np.float64)


E2M1 = np.array([0.0, 0.5, 1.0, 1.5, 2.0, 3.0, 4.0, 6.0, -0.0, -0.5, -1.0, -1.5, -2.0, -3.0, -4.0, -6.0])


def pack_weight(w, fmt):
    k, n = w.shape
    w = f64(bf(w)).reshape(k // 32, 32, n)
    amax = np.abs(w).max(1)
    if fmt == "e4m3":
        byte = np.frexp(amax)[1] - 1 + 127 - 7
    else:
        mant, ex = np.frexp(amax / 6.0)
        byte = np.where(mant > 0.5, ex, ex - 1) + 127
    byte = np.clip(np.where(amax > 0, byte, 1), 1, 254)
    scaled = (w * np.exp2(127.0 - byte)[:, None, :]).reshape(k, n).astype(np.float32)
    by_word = np.ascontiguousarray(scaled.reshape(k // 512, 128, 4, n).transpose(0, 1, 3, 2))
    if fmt == "e4m3":
        words = by_word.astype(ml_dtypes.float8_e4m3fn).view(np.uint8)
    else:
        c = by_word.astype(ml_dtypes.float4_e2m1fn).view(np.uint8) & 0xF
        words = c[..., 0::2] | (c[..., 1::2] << 4)
    return np.ascontiguousarray(words), np.ascontiguousarray(byte.astype(np.uint8).reshape(k // 512, 16, n))


def unpack_weight(words, scales, fmt):
    g, p, n, _ = words.shape
    if fmt == "e4m3":
        vals = np.ascontiguousarray(words).view(ml_dtypes.float8_e4m3fn).astype(np.float64)
    else:
        nib = np.empty((g, p, n, 4), np.uint8)
        nib[..., 0::2] = words & 0xF
        nib[..., 1::2] = words >> 4
        vals = E2M1[nib]
    vals = vals * np.repeat(np.exp2(scales.astype(np.float64) - 127.0), 8, axis=1)[..., None]
    return vals.transpose(0, 1, 3, 2).reshape(g * 512, n)

def pack4(w):
    words, scales = pack_weight(w, "e2m1")
    return words.reshape(words.shape[0], 128, -1), scales


def unpack4(words, scales):
    return unpack_weight(words.reshape(words.shape[0], 128, -1, 2), scales, "e2m1")


B, N, D, L = 1, 1024, 512, 512
SEGS = N // L


def setup_inputs():
    s = mx_kscale(D)
    col = np.concatenate([np.full(D, np.sqrt(SEGS)), np.ones(D)])
    x = bf(np.random.standard_normal((B, N, D)) * s)
    words, scales = pack4(np.random.standard_normal((D, D + D)) * col / np.sqrt(D) / s[:, None])
    return {"x": x, "w_kv_words": words, "w_kv_scales": scales}


def reference(x, w_kv_words, w_kv_scales):
    kv = mxq(f64(x), 2, "e5m2") @ unpack4(w_kv_words, w_kv_scales)
    k, v = kv[..., :D], kv[..., D:]
    keys_lm = k.reshape(B, L, SEGS, D).mean(axis=2)
    vals_lm = v.reshape(B, L, SEGS, D).mean(axis=2)
    return v, keys_lm, vals_lm

@@ -1,0 +1,134 @@
+from contextlib import ExitStack
+
+import concourse.mybir as mybir
+from concourse.masks import make_identity
+
+N_TOK, D = 1024, 512
+FLOPS = 2 * N_TOK * D * (2 * D)
+
+F32 = mybir.dt.float32
+BF16 = mybir.dt.bfloat16
+I32 = mybir.dt.int32
+U32 = mybir.dt.uint32
+U8 = mybir.dt.uint8
+E5M2X4 = mybir.dt.float8_e5m2_x4
+E2M1X4 = mybir.dt.float4_e2m1fn_x4
+MULT = mybir.AluOpType.mult
+ADD = mybir.AluOpType.add
+
+P = 128
+SEG = 2
+STEPS = N_TOK // (P * SEG)
+KEYS, VALUES = 0, 1
+
+
+def tile_ammattention_pa_kernel(tc, x, w_kv_words, w_kv_scales, out_0, out_1, out_2):
+    nc = tc.nc
+    x_rows = x[0].rearrange("(p j e) k -> p j e k", j=STEPS, e=SEG)
+    v_rows = out_0[0].rearrange("(p j e) n -> p j e n", j=STEPS, e=SEG)
+    key_rows = out_1[0].rearrange("(p j) n -> p j n", j=STEPS)
+    val_rows = out_2[0].rearrange("(p j) n -> p j n", j=STEPS)
+
+    with ExitStack() as ctx:
+        keep = ctx.enter_context(tc.tile_pool(name="keep", bufs=1))
+        psum = ctx.enter_context(tc.psum_pool(name="psum", bufs=8))
+        ctx.enter_context(tc.manual_schedule())
+
+        identity = keep.tile([P, P], F32)
+        make_identity(nc, identity[:])
+
+        w_scales = keep.tile([P, 2 * D], U8, align_bytes=64)
+        nc.vector.memset(w_scales[:].bitcast(I32), 0)
+        w_words = [keep.tile([P, 2 * D], U8, align_bytes=64, name="w_words%d" % h) for h in (KEYS, VALUES)]
+
+        x_sb = {}
+
+        def load_x(j, first, count):
+            t = keep.tile([P, count, D], BF16, name="x%d_%d" % (j, first))
+            nc.sync.dma_start(out=t[:], in_=x_rows[:, j, first : first + count, :])
+            for i in range(count):
+                x_sb[j, first + i] = t[:, i, :]
+
+        def load_w(h):
+            nc.sync.dma_start(out=w_words[h][:].bitcast(I32), in_=w_kv_words[0][:, 2 * D * h : 2 * D * (h + 1)].bitcast(I32))
+
+        load_x(0, 0, 1)
+        load_x(0, 1, 1)
+        load_w(VALUES)
+        for q in range(4):
+            nc.sync.dma_start(
+                out=w_scales[32 * q : 32 * q + 4, :].bitcast(I32),
+                in_=w_kv_scales[0][4 * q : 4 * q + 4, :].bitcast(I32),
+            )
+        load_x(1, 0, SEG)
+        load_w(KEYS)
+        for j in range(2, STEPS):
+            load_x(j, 0, SEG)
+
+        grouped, codes, scales = {}, {}, {}
+
+        def turn(j, copy):
+            banks = []
+            for e in range(SEG):
+                words = x_sb[j, e].bitcast(F32)
+                bank = psum.tile([P, 2, P], F32, name="bank")
+                for u in range(2):
+                    nc.tensor.transpose(bank[:, u, :], words[:, u : D // 2 : 2], identity[:])
+                banks.append(bank)
+            for e in range(SEG):
+                g = keep.tile([P, 4 * P], BF16, align_bytes=64, name="grouped%d_%d" % (j, e))
+                copy(out=g[:].bitcast(F32).rearrange("p (r u) -> p r u", u=2), in_=banks[e][:].rearrange("p u r -> p r u"))
+                grouped[j, e] = g
+
+        def quantise(j):
+            for e in range(SEG):
+                codes[j, e] = keep.tile([P, P], U32, align_bytes=64, name="codes%d_%d" % (j, e))
+                scales[j, e] = keep.tile([P, P], U8, align_bytes=64, name="scales%d_%d" % (j, e))
+                nc.vector.quantize_mx(out=codes[j, e][:].bitcast(E5M2X4), scales=scales[j, e][:], in_=grouped[j, e][:])
+
+        def multiply(bank, j, e, h, start, stop):
+            nc.tensor.matmul_mx(
+                out=bank[:],
+                lhsT=codes[j, e][:].bitcast(E5M2X4),
+                lhsT_scale=scales[j, e][:],
+                rhs=w_words[h][:].bitcast(E2M1X4),
+                rhs_scale=w_scales[:, D * h : D * (h + 1)],
+                start=start,
+                stop=stop,
+            )
+
+        turn(0, nc.scalar.copy)
+        quantise(0)
+        turn(1, nc.vector.tensor_copy)
+        quantise(1)
+
+        key_mean = keep.tile([P, STEPS, D], F32)
+        val_mean = keep.tile([P, STEPS, D], F32)
+        for j in range(STEPS):
+            early = j < 2
+            v_sb = keep.tile([P, SEG, D], F32, name="v%d" % j)
+            for e in range(SEG):
+                bank = psum.tile([P, D], F32, name="bank")
+                multiply(bank, j, e, VALUES, True, True)
+                nc.scalar.copy(out=v_sb[:, e, :], in_=bank[:])
+                if early:
+                    nc.sync.dma_start(out=v_rows[:, j, e, :], in_=v_sb[:, e, :])
+            if not early:
+                nc.sync.dma_start(out=v_rows[:, j, :, :], in_=v_sb[:])
+            key_bank = psum.tile([P, D], F32, name="bank")
+            for e in range(SEG):
+                multiply(key_bank, j, e, KEYS, e == 0, e == SEG - 1)
+            if j + 2 < STEPS:
+                turn(j + 2, nc.scalar.copy)
+
+            half = keep.tile([P, D], F32, name="half%d" % j)
+            nc.vector.tensor_scalar(out=half[:], in0=v_sb[:, 0, :], scalar1=0.5, scalar2=None, op0=MULT)
+            nc.vector.tensor_scalar(out=key_mean[:, j, :], in0=key_bank[:], scalar1=0.5, scalar2=None, op0=MULT)
+            nc.vector.scalar_tensor_tensor(out=val_mean[:, j, :], in0=v_sb[:, 1, :], scalar=0.5, in1=half[:], op0=MULT, op1=ADD)
+            if early:
+                nc.sync.dma_start(out=key_rows[:, j, :], in_=key_mean[:, j, :])
+                nc.sync.dma_start(out=val_rows[:, j, :], in_=val_mean[:, j, :])
+            if j + 2 < STEPS:
+                quantise(j + 2)
+        nc.sync.dma_start(out=key_rows[:, 2:, :], in_=key_mean[:, 2:, :])
+        nc.sync.dma_start(out=val_rows[:, 2:, :], in_=val_mean[:, 2:, :])

@@ -41,6 +41,12 @@ def tile_ammattention_pa_kernel(tc, x, w_kv_words, w_kv_scales, out_0, out_1, ou
         nc.vector.memset(w_scales[:].bitcast(I32), 0)
         w_words = [keep.tile([P, 2 * D], U8, align_bytes=64, name="w_words%d" % h) for h in (KEYS, VALUES)]
 
+        warm = keep.tile([P, D], BF16)
+        nc.vector.memset(warm[:].bitcast(I32), 0)
+        warm_bank = psum.tile([P, D], F32, name="bank")
+        for i in range(4):
+            nc.tensor.matmul(warm_bank[:], lhsT=warm[:, :P], rhs=warm[:], start=True, stop=True)
+
         x_sb = {}
 
         def load_x(j, first, count):

@@ -37,15 +37,15 @@ def tile_ammattention_pa_kernel(tc, x, w_kv_words, w_kv_scales, out_0, out_1, ou
         identity = keep.tile([P, P], F32)
         make_identity(nc, identity[:])
 
-        w_scales = keep.tile([P, 2 * D], U8, align_bytes=64)
-        nc.vector.memset(w_scales[:].bitcast(I32), 0)
-        w_words = [keep.tile([P, 2 * D], U8, align_bytes=64, name="w_words%d" % h) for h in (KEYS, VALUES)]
-
         warm = keep.tile([P, D], BF16)
         nc.vector.memset(warm[:].bitcast(I32), 0)
         warm_bank = psum.tile([P, D], F32, name="bank")
         for i in range(4):
             nc.tensor.matmul(warm_bank[:], lhsT=warm[:, :P], rhs=warm[:], start=True, stop=True)
+
+        w_scales = keep.tile([P, 2 * D], U8, align_bytes=64)
+        nc.vector.memset(w_scales[:].bitcast(I32), 0)
+        w_words = [keep.tile([P, 2 * D], U8, align_bytes=64, name="w_words%d" % h) for h in (KEYS, VALUES)]
 
         x_sb = {}
 
@@ -60,20 +60,20 @@ def tile_ammattention_pa_kernel(tc, x, w_kv_words, w_kv_scales, out_0, out_1, ou
 
         load_x(0, 0, 1)
         load_x(0, 1, 1)
-        load_w(VALUES)
+        load_x(1, 0, SEG)
         for q in range(4):
             nc.sync.dma_start(
                 out=w_scales[32 * q : 32 * q + 4, :].bitcast(I32),
                 in_=w_kv_scales[0][4 * q : 4 * q + 4, :].bitcast(I32),
             )
-        load_x(1, 0, SEG)
+        load_w(VALUES)
         load_w(KEYS)
         for j in range(2, STEPS):
             load_x(j, 0, SEG)
 
         grouped, codes, scales = {}, {}, {}
 
-        def turn(j, copy):
+        def turn(j, copies):
             banks = []
             for e in range(SEG):
                 words = x_sb[j, e].bitcast(F32)
@@ -83,7 +83,7 @@ def tile_ammattention_pa_kernel(tc, x, w_kv_words, w_kv_scales, out_0, out_1, ou
                 banks.append(bank)
             for e in range(SEG):
                 g = keep.tile([P, 4 * P], BF16, align_bytes=64, name="grouped%d_%d" % (j, e))
-                copy(out=g[:].bitcast(F32).rearrange("p (r u) -> p r u", u=2), in_=banks[e][:].rearrange("p u r -> p r u"))
+                copies[e](out=g[:].bitcast(F32).rearrange("p (r u) -> p r u", u=2), in_=banks[e][:].rearrange("p u r -> p r u"))
                 grouped[j, e] = g
 
         def quantise(j):
@@ -92,21 +92,22 @@ def tile_ammattention_pa_kernel(tc, x, w_kv_words, w_kv_scales, out_0, out_1, ou
                 scales[j, e] = keep.tile([P, P], U8, align_bytes=64, name="scales%d_%d" % (j, e))
                 nc.vector.quantize_mx(out=codes[j, e][:].bitcast(E5M2X4), scales=scales[j, e][:], in_=grouped[j, e][:])
 
-        def multiply(bank, j, e, h, start, stop):
+        def multiply(bank, j, e, h, start, stop, first=0, width=D):
             nc.tensor.matmul_mx(
                 out=bank[:],
                 lhsT=codes[j, e][:].bitcast(E5M2X4),
                 lhsT_scale=scales[j, e][:],
-                rhs=w_words[h][:].bitcast(E2M1X4),
-                rhs_scale=w_scales[:, D * h : D * (h + 1)],
+                rhs=w_words[h][:, 2 * first : 2 * (first + width)].bitcast(E2M1X4),
+                rhs_scale=w_scales[:, D * h + first : D * h + first + width],
                 start=start,
                 stop=stop,
             )
 
-        turn(0, nc.scalar.copy)
+        on_scalar = (nc.scalar.copy, nc.scalar.copy)
+        on_both = (nc.scalar.copy, nc.vector.tensor_copy)
+        turn(0, on_scalar)
         quantise(0)
-        turn(1, nc.vector.tensor_copy)
-        quantise(1)
+        turn(1, on_both)
 
         key_mean = keep.tile([P, STEPS, D], F32)
         val_mean = keep.tile([P, STEPS, D], F32)
@@ -114,9 +115,14 @@ def tile_ammattention_pa_kernel(tc, x, w_kv_words, w_kv_scales, out_0, out_1, ou
             early = j < 2
             v_sb = keep.tile([P, SEG, D], F32, name="v%d" % j)
             for e in range(SEG):
-                bank = psum.tile([P, D], F32, name="bank")
-                multiply(bank, j, e, VALUES, True, True)
-                nc.scalar.copy(out=v_sb[:, e, :], in_=bank[:])
+                copies = on_both if (j, e) == (0, 0) else on_scalar[:1]
+                width = D // len(copies)
+                for i, copy in enumerate(copies):
+                    bank = psum.tile([P, width], F32, name="bank")
+                    multiply(bank, j, e, VALUES, True, True, i * width, width)
+                    copy(out=v_sb[:, e, i * width : (i + 1) * width], in_=bank[:])
+                if (j, e) == (0, 0):
+                    quantise(1)
                 if early:
                     nc.sync.dma_start(out=v_rows[:, j, e, :], in_=v_sb[:, e, :])
             if not early:
@@ -125,7 +131,7 @@ def tile_ammattention_pa_kernel(tc, x, w_kv_words, w_kv_scales, out_0, out_1, ou
             for e in range(SEG):
                 multiply(key_bank, j, e, KEYS, e == 0, e == SEG - 1)
             if j + 2 < STEPS:
-                turn(j + 2, nc.scalar.copy)
+                turn(j + 2, on_scalar)
 
             half = keep.tile([P, D], F32, name="half%d" % j)
             nc.vector.tensor_scalar(out=half[:], in0=v_sb[:, 0, :], scalar1=0.5, scalar2=None, op0=MULT)

from contextlib import ExitStack

import concourse.mybir as mybir
from concourse.masks import make_identity

N_TOK, D = 1024, 512
FLOPS = 2 * N_TOK * D * (2 * D)

F32 = mybir.dt.float32
BF16 = mybir.dt.bfloat16
I32 = mybir.dt.int32
U32 = mybir.dt.uint32
U8 = mybir.dt.uint8
E5M2X4 = mybir.dt.float8_e5m2_x4
E2M1X4 = mybir.dt.float4_e2m1fn_x4
MULT = mybir.AluOpType.mult
ADD = mybir.AluOpType.add

P = 128
SEG = 2
STEPS = N_TOK // (P * SEG)
KEYS, VALUES = 0, 1


def tile_ammattention_pa_kernel(tc, x, w_kv_words, w_kv_scales, out_0, out_1, out_2):
    nc = tc.nc
    x_rows = x[0].rearrange("(p j e) k -> p j e k", j=STEPS, e=SEG)
    v_rows = out_0[0].rearrange("(p j e) n -> p j e n", j=STEPS, e=SEG)
    key_rows = out_1[0].rearrange("(p j) n -> p j n", j=STEPS)
    val_rows = out_2[0].rearrange("(p j) n -> p j n", j=STEPS)

    with ExitStack() as ctx:
        keep = ctx.enter_context(tc.tile_pool(name="keep", bufs=1))
        psum = ctx.enter_context(tc.psum_pool(name="psum", bufs=8))
        ctx.enter_context(tc.manual_schedule())

        identity = keep.tile([P, P], F32)
        make_identity(nc, identity[:])

        warm = keep.tile([P, D], BF16)
        nc.vector.memset(warm[:].bitcast(I32), 0)
        warm_bank = psum.tile([P, D], F32, name="bank")
        for i in range(4):
            nc.tensor.matmul(warm_bank[:], lhsT=warm[:, :P], rhs=warm[:], start=True, stop=True)

        w_scales = keep.tile([P, 2 * D], U8, align_bytes=64)
        nc.vector.memset(w_scales[:].bitcast(I32), 0)
        w_words = [keep.tile([P, 2 * D], U8, align_bytes=64, name="w_words%d" % h) for h in (KEYS, VALUES)]

        x_sb = {}

        def load_x(j, first, count):
            t = keep.tile([P, count, D], BF16, name="x%d_%d" % (j, first))
            nc.sync.dma_start(out=t[:], in_=x_rows[:, j, first : first + count, :])
            for i in range(count):
                x_sb[j, first + i] = t[:, i, :]

        def load_w(h):
            nc.sync.dma_start(out=w_words[h][:].bitcast(I32), in_=w_kv_words[0][:, 2 * D * h : 2 * D * (h + 1)].bitcast(I32))

        load_x(0, 0, 1)
        load_x(0, 1, 1)
        load_x(1, 0, SEG)
        for q in range(4):
            nc.sync.dma_start(
                out=w_scales[32 * q : 32 * q + 4, :].bitcast(I32),
                in_=w_kv_scales[0][4 * q : 4 * q + 4, :].bitcast(I32),
            )
        load_w(VALUES)
        load_w(KEYS)
        for j in range(2, STEPS):
            load_x(j, 0, SEG)

        grouped, codes, scales = {}, {}, {}

        def turn(j, copies):
            banks = []
            for e in range(SEG):
                words = x_sb[j, e].bitcast(F32)
                bank = psum.tile([P, 2, P], F32, name="bank")
                for u in range(2):
                    nc.tensor.transpose(bank[:, u, :], words[:, u : D // 2 : 2], identity[:])
                banks.append(bank)
            for e in range(SEG):
                g = keep.tile([P, 4 * P], BF16, align_bytes=64, name="grouped%d_%d" % (j, e))
                copies[e](out=g[:].bitcast(F32).rearrange("p (r u) -> p r u", u=2), in_=banks[e][:].rearrange("p u r -> p r u"))
                grouped[j, e] = g

        def quantise(j):
            for e in range(SEG):
                codes[j, e] = keep.tile([P, P], U32, align_bytes=64, name="codes%d_%d" % (j, e))
                scales[j, e] = keep.tile([P, P], U8, align_bytes=64, name="scales%d_%d" % (j, e))
                nc.vector.quantize_mx(out=codes[j, e][:].bitcast(E5M2X4), scales=scales[j, e][:], in_=grouped[j, e][:])

        def multiply(bank, j, e, h, start, stop, first=0, width=D):
            nc.tensor.matmul_mx(
                out=bank[:],
                lhsT=codes[j, e][:].bitcast(E5M2X4),
                lhsT_scale=scales[j, e][:],
                rhs=w_words[h][:, 2 * first : 2 * (first + width)].bitcast(E2M1X4),
                rhs_scale=w_scales[:, D * h + first : D * h + first + width],
                start=start,
                stop=stop,
            )

        on_scalar = (nc.scalar.copy, nc.scalar.copy)
        on_both = (nc.scalar.copy, nc.vector.tensor_copy)
        turn(0, on_scalar)
        quantise(0)
        turn(1, on_both)

        key_mean = keep.tile([P, STEPS, D], F32)
        val_mean = keep.tile([P, STEPS, D], F32)
        for j in range(STEPS):
            early = j < 2
            v_sb = keep.tile([P, SEG, D], F32, name="v%d" % j)
            for e in range(SEG):
                copies = on_both if (j, e) == (0, 0) else on_scalar[:1]
                width = D // len(copies)
                for i, copy in enumerate(copies):
                    bank = psum.tile([P, width], F32, name="bank")
                    multiply(bank, j, e, VALUES, True, True, i * width, width)
                    copy(out=v_sb[:, e, i * width : (i + 1) * width], in_=bank[:])
                if (j, e) == (0, 0):
                    quantise(1)
                if early:
                    nc.sync.dma_start(out=v_rows[:, j, e, :], in_=v_sb[:, e, :])
            if not early:
                nc.sync.dma_start(out=v_rows[:, j, :, :], in_=v_sb[:])
            key_bank = psum.tile([P, D], F32, name="bank")
            for e in range(SEG):
                multiply(key_bank, j, e, KEYS, e == 0, e == SEG - 1)
            if j + 2 < STEPS:
                turn(j + 2, on_scalar)

            half = keep.tile([P, D], F32, name="half%d" % j)
            nc.vector.tensor_scalar(out=half[:], in0=v_sb[:, 0, :], scalar1=0.5, scalar2=None, op0=MULT)
            nc.vector.tensor_scalar(out=key_mean[:, j, :], in0=key_bank[:], scalar1=0.5, scalar2=None, op0=MULT)
            nc.vector.scalar_tensor_tensor(out=val_mean[:, j, :], in0=v_sb[:, 1, :], scalar=0.5, in1=half[:], op0=MULT, op1=ADD)
            if early:
                nc.sync.dma_start(out=key_rows[:, j, :], in_=key_mean[:, j, :])
                nc.sync.dma_start(out=val_rows[:, j, :], in_=val_mean[:, j, :])
            if j + 2 < STEPS:
                quantise(j + 2)
        nc.sync.dma_start(out=key_rows[:, 2:, :], in_=key_mean[:, 2:, :])
        nc.sync.dma_start(out=val_rows[:, 2:, :], in_=val_mean[:, 2:, :])
